import numpy as np
import ml_dtypes


def mxq(x, axis, fmt="e4m3"):
    dtype, down = {"e4m3": (ml_dtypes.float8_e4m3fn, 7), "e5m2": (ml_dtypes.float8_e5m2, 14)}[fmt]
    v = np.moveaxis(np.asarray(x, np.float32).astype(ml_dtypes.bfloat16).astype(np.float64), axis, -1)
    blocks = v.reshape(v.shape[:-1] + (-1, 32))
    amax = np.abs(blocks).max(-1, keepdims=True)
    byte = np.maximum(np.where(amax > 0, np.frexp(amax)[1] - 1 + 127, 0) - down, 1)
    scale = np.exp2(byte - 127.0)
    codes = (blocks / scale).astype(np.float32).astype(dtype).astype(np.float64)
    return np.moveaxis((codes * scale).reshape(v.shape), -1, axis)


WIDE = False


def mx_kscale(k):
    if not WIDE:
        return np.ones(k)
    levels = np.array([10, -10, 5, -5, 0])
    a = np.random.permutation(np.resize(levels, k // 512 * 4)).reshape(k // 512, 4)
    idx = np.arange(k)
    return np.exp2(a[idx // 512, idx % 128 // 32])


BF16 = ml_dtypes.bfloat16


def bf(x):
    return np.asarray(x, np.float32).astype(BF16)


def f64(x):
    return np.asarray(x).astype(np.float64)


B, D, H, W, K = 4, 1024, 64, 64, 128
N = H * W
EPS = 1e-08


def softmax(v):
    e = np.exp(v - v.max(-1, keepdims=True))
    return e / e.sum(-1, keepdims=True)


def setup_inputs():
    s = mx_kscale(D)
    return {"x": bf(np.random.standard_normal((B, D, H, W)) * s[None, :, None, None]),
            "conv_w": bf(np.random.standard_normal((K, D)) * np.sqrt(2.0 / D) / s[None, :]),
            "centroids": bf(np.random.standard_normal((K, D)) * np.sqrt(2.0 / D) * s[None, :])}


def reference(x, conv_w, centroids):
    d = f64(x).reshape(B, D, N).transpose(0, 2, 1)
    logits = (mxq(d, 2, "e4m3") @ mxq(f64(conv_w), 1, "e4m3").T) + EPS
    w = softmax(logits)
    vlad = (mxq(w, 1, "e4m3").transpose(0, 2, 1) @ mxq(d, 1, "e4m3")) - w.sum(1)[..., None] * f64(centroids)[None]
    return vlad.reshape(B, -1)

@@ -1,0 +1,181 @@
+from contextlib import ExitStack
+
+import concourse.bass as bass
+import concourse.mybir as mybir
+import concourse.tile as tile
+from concourse.masks import make_identity
+
+F32 = mybir.dt.float32
+BF16 = mybir.dt.bfloat16
+U32 = mybir.dt.uint32
+U8 = mybir.dt.uint8
+FP8X4 = mybir.dt.float8_e4m3fn_x4
+ALU = mybir.AluOpType
+ACT = mybir.ActivationFunctionType
+AX = mybir.AxisListType
+
+P = 128
+B = 4
+D = 1024
+N = 4096
+K = 128
+STEP = 512
+FLOPS = 2 * 2 * B * N * D * K
+
+
+def tile_netvlad_t_kernel(tc, x, conv_w, centroids, out):
+    nc = tc.nc
+    with ExitStack() as ctx:
+        const = ctx.enter_context(tc.tile_pool(name="const", bufs=1))
+        xpool = ctx.enter_context(tc.tile_pool(name="xpool", bufs=4))
+        work = ctx.enter_context(tc.tile_pool(name="work", bufs=3))
+        small = ctx.enter_context(tc.tile_pool(name="small", bufs=4))
+        respool = ctx.enter_context(tc.tile_pool(name="respool", bufs=2))
+        ps_l = ctx.enter_context(tc.psum_pool(name="ps_l", bufs=2))
+        ps_t = ctx.enter_context(tc.psum_pool(name="ps_t", bufs=3))
+        ps_a = ctx.enter_context(tc.psum_pool(name="ps_a", bufs=1))
+
+        ident = const.tile([P, P], F32)
+        make_identity(nc, ident[:])
+
+        cw_sb = const.tile([P, D], BF16)
+        nc.sync.dma_start(out=cw_sb[:], in_=conv_w)
+        cent = const.tile([P, D], BF16)
+        nc.gpsimd.dma_start(out=cent[:], in_=centroids)
+        cw_w = cw_sb[:].bitcast(F32).rearrange("p (h q i) -> p h i q", h=2, q=P, i=2)
+        cw_t = ps_t.tile([P, 2, 2, P], F32, tag="tr")
+        for h in range(2):
+            for i in range(2):
+                nc.tensor.transpose(cw_t[:, h, i, :], cw_w[:, h, i, :], ident[:])
+        cw_g = const.tile([P, D], BF16, align_bytes=64)
+        nc.vector.tensor_copy(
+            out=cw_g[:].bitcast(F32).rearrange("p (h k i) -> p h k i", h=2, k=K, i=2),
+            in_=cw_t[:].rearrange("p h i k -> p h k i"),
+        )
+        cw_codes = const.tile([P, 2 * K], U32, align_bytes=64)
+        cw_scales = const.tile([P, 2 * K], U8, align_bytes=64)
+        nc.vector.quantize_mx(out=cw_codes[:].bitcast(FP8X4), scales=cw_scales[:], in_=cw_g[:])
+
+        for b in range(B):
+            xv = x[b].rearrange("(h p j) a w -> h p j (a w)", h=2, p=P, j=4)
+            widths = [512, 512, 1024, 1024, 1024] if b == 0 else [1024] * 4
+            acc = [
+                ps_a.tile([P, STEP], F32, name="acc0", tag="acc0"),
+                ps_a.tile([P, STEP], F32, name="acc1", tag="acc1"),
+            ]
+            wsum_ps = ps_a.tile([P, K], F32, tag="wsum")
+            n0 = 0
+            for width in widths:
+                xs = xpool.tile([P, 8 * 1024], BF16, tag="xs")
+                xs_b = xs[:, 0 : 8 * width].rearrange("p (c n) -> p c n", c=8)
+                xs_w = xs[:, 0 : 8 * width].bitcast(F32).rearrange("p (c m) -> p c m", c=8)
+                for h in range(2):
+                    nc.sync.dma_start(out=xs_b[:, 4 * h : 4 * h + 4, :], in_=xv[h][:, :, n0 : n0 + width])
+                for o in range(0, width, STEP):
+                    g = (n0 + o) // STEP
+                    g1 = work.tile([P, 2, STEP, 4], BF16, align_bytes=64)
+                    nc.vector.tensor_copy(
+                        out=g1[:, 0].rearrange("p (u e q) j -> p u q j e", u=2, e=2, q=P),
+                        in_=xs_b[:, 0:4, o : o + STEP].rearrange("p j (u q e) -> p u q j e", u=2, e=2, q=P),
+                    )
+                    for u in range(2):
+                        nc.scalar.copy(
+                            out=g1[:, 1, 256 * u : 256 * u + 256, :].rearrange("p (e q) j -> p q j e", e=2, q=P),
+                            in_=xs_b[:, 4:8, o + 256 * u : o + 256 * u + 256].rearrange("p j (q e) -> p q j e", e=2, q=P),
+                        )
+                    c1 = work.tile([P, 2 * STEP], U32, align_bytes=64)
+                    s1 = work.tile([P, 2 * STEP], U8, align_bytes=64)
+                    for h in range(2):
+                        nc.vector.quantize_mx(
+                            out=c1[:, STEP * h : STEP * h + STEP].bitcast(FP8X4),
+                            scales=s1[:, STEP * h : STEP * h + STEP],
+                            in_=g1[:, h].rearrange("p n j -> p (n j)"),
+                        )
+                    lg = ps_l.tile([P, 4, K], F32)
+                    for t in range(4):
+                        for h in range(2):
+                            cols = slice(STEP * h + P * t, STEP * h + P * t + P)
+                            nc.tensor.matmul_mx(
+                                out=lg[:, t, :],
+                                lhsT=c1[:, cols].bitcast(FP8X4),
+                                lhsT_scale=s1[:, cols],
+                                rhs=cw_codes[:, K * h : K * h + K].bitcast(FP8X4),
+                                rhs_scale=cw_scales[:, K * h : K * h + K],
+                                start=(h == 0),
+                                stop=(h == 1),
+                            )
+                    nmx = small.tile([P, 4], F32)
+                    nc.vector.tensor_reduce(out=nmx[:], in_=lg[:], axis=AX.X, op=ALU.max, negate=True)
+                    ex = work.tile([P, 4, K], F32)
+                    ssum = small.tile([P, 4], F32)
+                    for t in range(4):
+                        nc.scalar.activation(
+                            out=ex[:, t, :], in_=lg[:, t, :], func=ACT.Exp,
+                            bias=nmx[:, t : t + 1], scale=1.0, accum_out=ssum[:, t : t + 1],
+                        )
+                    rinv = small.tile([P, 4], F32)
+                    nc.vector.reciprocal(out=rinv[:], in_=ssum[:])
+                    gw = work.tile([P, K, 4], BF16, align_bytes=64)
+                    nc.vector.tensor_tensor(
+                        out=gw[:],
+                        in0=ex[:].rearrange("p t k -> p k t"),
+                        in1=rinv[:].unsqueeze(1).to_broadcast([P, K, 4]),
+                        op=ALU.mult,
+                    )
+                    cq = work.tile([P, K], U32, align_bytes=64)
+                    sq = work.tile([P, K], U8, align_bytes=64)
+                    nc.vector.quantize_mx(
+                        out=cq[:].bitcast(FP8X4), scales=sq[:], in_=gw[:].rearrange("p k t -> p (k t)")
+                    )
+                    for t in range(4):
+                        nc.tensor.matmul(
+                            out=wsum_ps[:],
+                            lhsT=rinv[:, t : t + 1].to_broadcast([P, P]),
+                            rhs=ex[:, t, :],
+                            start=(g == 0 and t == 0),
+                            stop=(g == N // STEP - 1 and t == 3),
+                        )
+                    g2 = work.tile([P, 4 * D], BF16, align_bytes=64)
+                    g2_w = g2[:].bitcast(F32).rearrange("p (c u) -> p c u", u=2)
+                    for i in range(4):
+                        tr = ps_t.tile([P, 2, 2, P], F32, tag="tr")
+                        for u in range(2):
+                            for cb in range(2):
+                                m0 = o // 2 + P * u
+                                nc.tensor.transpose(tr[:, u, cb, :], xs_w[:, 2 * i + cb, m0 : m0 + P], ident[:])
+                        nc.scalar.copy(
+                            out=g2_w[:, 256 * i : 256 * i + 256, :],
+                            in_=tr[:].rearrange("p u c q -> p (c q) u"),
+                        )
+                    c2 = work.tile([P, D], U32, align_bytes=64)
+                    s2 = work.tile([P, D], U8, align_bytes=64)
+                    nc.vector.quantize_mx(out=c2[:].bitcast(FP8X4), scales=s2[:], in_=g2[:])
+                    for h in range(2):
+                        nc.tensor.matmul_mx(
+                            out=acc[h][:],
+                            lhsT=cq[:].bitcast(FP8X4),
+                            lhsT_scale=sq[:],
+                            rhs=c2[:, STEP * h : STEP * h + STEP].bitcast(FP8X4),
+                            rhs_scale=s2[:, STEP * h : STEP * h + STEP],
+                            start=(g == 0),
+                            stop=(g == N // STEP - 1),
+                        )
+                n0 += width
+            ws_sb = small.tile([P, K], F32)
+            nc.vector.tensor_copy(out=ws_sb[:], in_=wsum_ps[:])
+            ws_t = ps_t.tile([P, P], F32, tag="tr")
+            nc.tensor.transpose(ws_t[:], ws_sb[:], ident[:])
+            nws = small.tile([P, 1], F32)
+            nc.vector.tensor_scalar_mul(out=nws[:], in0=ws_t[:, 0:1], scalar1=-1.0)
+            res = respool.tile([P, D], F32)
+            for h in range(2):
+                nc.vector.scalar_tensor_tensor(
+                    out=res[:, STEP * h : STEP * h + STEP].rearrange("p (q j) -> p q j", j=4),
+                    in0=cent[:, STEP * h : STEP * h + STEP].rearrange("p (q j) -> p q j", j=4),
+                    scalar=nws[:, 0:1],
+                    in1=acc[h][:].rearrange("p (j q) -> p q j", j=4),
+                    op0=ALU.mult,
+                    op1=ALU.add,
+                )
+            store = nc.sync if b == B - 1 else nc.gpsimd
+            store.dma_start(out=out[b].rearrange("(k c) -> k c", k=K), in_=res[:])

@@ -1,8 +1,6 @@
 from contextlib import ExitStack
 
-import concourse.bass as bass
 import concourse.mybir as mybir
-import concourse.tile as tile
 from concourse.masks import make_identity
 
 F32 = mybir.dt.float32
@@ -20,6 +18,10 @@ D = 1024
 N = 4096
 K = 128
 STEP = 512
+SPB = N // STEP
+NS = B * SPB
+XBUFS = 5
+VQ = 64
 FLOPS = 2 * 2 * B * N * D * K
 
 
@@ -27,23 +29,254 @@ def tile_netvlad_t_kernel(tc, x, conv_w, centroids, out):
     nc = tc.nc
     with ExitStack() as ctx:
         const = ctx.enter_context(tc.tile_pool(name="const", bufs=1))
-        xpool = ctx.enter_context(tc.tile_pool(name="xpool", bufs=4))
-        work = ctx.enter_context(tc.tile_pool(name="work", bufs=3))
-        small = ctx.enter_context(tc.tile_pool(name="small", bufs=4))
+        xpool = ctx.enter_context(tc.tile_pool(name="xpool", bufs=XBUFS))
+        gpool = ctx.enter_context(tc.tile_pool(name="gpool", bufs=3))
+        qpool = ctx.enter_context(tc.tile_pool(name="qpool", bufs=2))
+        small = ctx.enter_context(tc.tile_pool(name="small", bufs=3))
         respool = ctx.enter_context(tc.tile_pool(name="respool", bufs=2))
-        ps_l = ctx.enter_context(tc.psum_pool(name="ps_l", bufs=2))
-        ps_t = ctx.enter_context(tc.psum_pool(name="ps_t", bufs=3))
+        ps_l = ctx.enter_context(tc.psum_pool(name="ps_l", bufs=1))
+        ps_t = ctx.enter_context(tc.psum_pool(name="ps_t", bufs=4))
         ps_a = ctx.enter_context(tc.psum_pool(name="ps_a", bufs=1))
+        ctx.enter_context(tc.manual_schedule())
 
-        ident = const.tile([P, P], F32)
-        make_identity(nc, ident[:])
+        st = {}
+        chunks = [(0, 0, 512), (0, 512, 512), (0, 1024, 1024), (0, 2048, 1024), (0, 3072, 1024)]
+        for b in range(1, B):
+            chunks.extend([(b, n0, 1024) for n0 in range(0, N, 1024)])
+        where = {}
+        last_step = {}
+        for ci, (b, n0, width) in enumerate(chunks):
+            for o in range(0, width, STEP):
+                where[b * SPB + (n0 + o) // STEP] = (ci, o)
+                last_step[ci] = b * SPB + (n0 + o) // STEP
 
         cw_sb = const.tile([P, D], BF16)
-        nc.sync.dma_start(out=cw_sb[:], in_=conv_w)
         cent = const.tile([P, D], BF16)
+
+        def load(ci):
+            b, n0, width = chunks[ci]
+            xv = x[b].rearrange("(h p j) a w -> h p j (a w)", h=2, p=P, j=4)
+            xs = xpool.tile([P, 8 * 1024], BF16, name="xs", tag="xs")
+            xs_b = xs[:, 0 : 8 * width].rearrange("p (c n) -> p c n", c=8)
+            for h in (1, 0):
+                nc.sync.dma_start(out=xs_b[:, 4 * h : 4 * h + 4, :], in_=xv[h][:, :, n0 : n0 + width])
+                if ci == 0 and h == 1:
+                    nc.sync.dma_start(out=cw_sb[:], in_=conv_w)
+            st[("xb", ci)] = xs_b
+            st[("xw", ci)] = xs[:, 0 : 8 * width].bitcast(F32).rearrange("p (c m) -> p c m", c=8)
+
+        def r1_views(s, h, u):
+            ci, o = where[s]
+            dst = st[("g1", s)][:, h, 256 * u : 256 * u + 256, :].rearrange("p (e q) j -> p q j e", e=2, q=P)
+            src = st[("xb", ci)][:, 4 * h : 4 * h + 4, o + 256 * u : o + 256 * u + 256].rearrange(
+                "p j (q e) -> p q j e", e=2, q=P
+            )
+            return dst, src
+
+        def r1_scalar(s):
+            if not 0 <= s < NS:
+                return
+            st[("g1", s)] = gpool.tile([P, 2, STEP, 4], BF16, name="g1", tag="g1", align_bytes=64)
+            dst, src = r1_views(s, 1, 0)
+            if VQ < P:
+                nc.scalar.copy(out=dst[:, VQ:P], in_=src[:, VQ:P])
+            dst, src = r1_views(s, 1, 1)
+            nc.scalar.copy(out=dst, in_=src)
+
+        def r1_vector(s):
+            if not 0 <= s < NS:
+                return
+            ci, o = where[s]
+            nc.vector.tensor_copy(
+                out=st[("g1", s)][:, 0].rearrange("p (u e q) j -> p u q j e", u=2, e=2, q=P),
+                in_=st[("xb", ci)][:, 0:4, o : o + STEP].rearrange("p j (u q e) -> p u q j e", u=2, e=2, q=P),
+            )
+            if VQ > 0:
+                dst, src = r1_views(s, 1, 0)
+                nc.vector.tensor_copy(out=dst[:, 0:VQ], in_=src[:, 0:VQ])
+
+        def q1(s):
+            if not 0 <= s < NS:
+                return
+            c1 = qpool.tile([P, 2 * STEP], U32, name="c1", tag="c1", align_bytes=64)
+            s1 = qpool.tile([P, 2 * STEP], U8, name="s1", tag="s1", align_bytes=64)
+            for h in range(2):
+                nc.vector.quantize_mx(
+                    out=c1[:, STEP * h : STEP * h + STEP].bitcast(FP8X4),
+                    scales=s1[:, STEP * h : STEP * h + STEP],
+                    in_=st[("g1", s)][:, h].rearrange("p n j -> p (n j)"),
+                )
+            st[("c1", s)] = (c1, s1)
+
+        def mm1(s):
+            if not 0 <= s < NS:
+                return
+            c1, s1 = st[("c1", s)]
+            lg = ps_l.tile([P, 4, K], F32, name="lg", tag="lg")
+            for t in range(4):
+                for h in range(2):
+                    cols = slice(STEP * h + P * t, STEP * h + P * t + P)
+                    nc.tensor.matmul_mx(
+                        out=lg[:, t, :],
+                        lhsT=c1[:, cols].bitcast(FP8X4),
+                        lhsT_scale=s1[:, cols],
+                        rhs=cw_codes[:, K * h : K * h + K].bitcast(FP8X4),
+                        rhs_scale=cw_scales[:, K * h : K * h + K],
+                        start=(h == 0),
+                        stop=(h == 1),
+                    )
+            st[("lg", s)] = lg
+
+        def vmax(s):
+            if not 0 <= s < NS:
+                return
+            nmx = small.tile([P, 4], F32, name="nmx", tag="nmx")
+            nc.vector.tensor_reduce(out=nmx[:], in_=st[("lg", s)][:], axis=AX.X, op=ALU.max, negate=True)
+            st[("nmx", s)] = nmx
+
+        def sexp(s):
+            if not 0 <= s < NS:
+                return
+            ex = qpool.tile([P, 4, K], F32, name="ex", tag="ex")
+            ssum = small.tile([P, 4], F32, name="ssum", tag="ssum")
+            for t in range(4):
+                nc.scalar.activation(
+                    out=ex[:, t, :], in_=st[("lg", s)][:, t, :], func=ACT.Exp,
+                    bias=st[("nmx", s)][:, t : t + 1], scale=1.0, accum_out=ssum[:, t : t + 1],
+                )
+            st[("ex", s)] = (ex, ssum)
+
+        def norm(s):
+            if not 0 <= s < NS:
+                return
+            ex, ssum = st[("ex", s)]
+            rinv = small.tile([P, 4], F32, name="rinv", tag="rinv")
+            nc.vector.reciprocal(out=rinv[:], in_=ssum[:])
+            gw = qpool.tile([P, K, 4], BF16, name="gw", tag="gw", align_bytes=64)
+            nc.vector.tensor_tensor(
+                out=gw[:],
+                in0=ex[:].rearrange("p t k -> p k t"),
+                in1=rinv[:].unsqueeze(1).to_broadcast([P, K, 4]),
+                op=ALU.mult,
+            )
+            st[("gw", s)] = (gw, rinv)
+
+        def qw(s):
+            if not 0 <= s < NS:
+                return
+            cq = qpool.tile([P, K], U32, name="cq", tag="cq", align_bytes=64)
+            sq = qpool.tile([P, K], U8, name="sq", tag="sq", align_bytes=64)
+            nc.vector.quantize_mx(
+                out=cq[:].bitcast(FP8X4), scales=sq[:], in_=st[("gw", s)][0][:].rearrange("p k t -> p (k t)")
+            )
+            st[("cq", s)] = (cq, sq)
+
+        def wsum(s):
+            if not 0 <= s < NS:
+                return
+            b, g = divmod(s, SPB)
+            if g == 0:
+                st[("ws", b)] = ps_a.tile([P, 2, K], F32, name="ws", tag="ws")
+            ex = st[("ex", s)][0]
+            rinv = st[("gw", s)][1]
+            for t in range(4):
+                nc.tensor.matmul(
+                    out=st[("ws", b)][:, 0, :],
+                    lhsT=rinv[:, t : t + 1].to_broadcast([P, P]),
+                    rhs=ex[:, t, :],
+                    start=(g == 0 and t == 0),
+                    stop=(g == SPB - 1 and t == 3),
+                )
+
+        def tr_r2(s):
+            if not 0 <= s < NS:
+                return
+            ci, o = where[s]
+            xs_w = st[("xw", ci)]
+            g2 = gpool.tile([P, 4 * D], BF16, name="g2", tag="g2", align_bytes=64)
+            g2_w = g2[:].bitcast(F32).rearrange("p (c u) -> p c u", u=2)
+            for i in range(4):
+                tr = ps_t.tile([P, 2, 2, P], F32, name="tr", tag="tr")
+                for u in range(2):
+                    for cb in range(2):
+                        m0 = o // 2 + P * u
+                        nc.tensor.transpose(tr[:, u, cb, :], xs_w[:, 2 * i + cb, m0 : m0 + P], ident[:])
+                nc.scalar.copy(
+                    out=g2_w[:, 256 * i : 256 * i + 256, :], in_=tr[:].rearrange("p u c q -> p (c q) u")
+                )
+            st[("g2", s)] = g2
+
+        def q2(s):
+            if not 0 <= s < NS:
+                return
+            c2 = qpool.tile([P, D], U32, name="c2", tag="c2", align_bytes=64)
+            s2 = qpool.tile([P, D], U8, name="s2", tag="s2", align_bytes=64)
+            nc.vector.quantize_mx(out=c2[:].bitcast(FP8X4), scales=s2[:], in_=st[("g2", s)][:])
+            st[("c2", s)] = (c2, s2)
+
+        def mm2(s):
+            if not 0 <= s < NS:
+                return
+            b, g = divmod(s, SPB)
+            if g == 0:
+                st[("acc", b)] = [
+                    ps_a.tile([P, STEP], F32, name="acc0", tag="acc0"),
+                    ps_a.tile([P, STEP], F32, name="acc1", tag="acc1"),
+                ]
+            cq, sq = st[("cq", s)]
+            c2, s2 = st[("c2", s)]
+            for h in range(2):
+                nc.tensor.matmul_mx(
+                    out=st[("acc", b)][h][:],
+                    lhsT=cq[:].bitcast(FP8X4),
+                    lhsT_scale=sq[:],
+                    rhs=c2[:, STEP * h : STEP * h + STEP].bitcast(FP8X4),
+                    rhs_scale=s2[:, STEP * h : STEP * h + STEP],
+                    start=(g == 0),
+                    stop=(g == SPB - 1),
+                )
+
+        def fin_copy(b):
+            ws_sb = small.tile([P, K], F32, name="ws_sb", tag="ws_sb")
+            nc.vector.tensor_copy(out=ws_sb[:], in_=st[("ws", b)][:, 0, :])
+            st[("ws_sb", b)] = ws_sb
+
+        def fin_tr(b):
+            nc.tensor.transpose(st[("ws", b)][:, 1, :], st[("ws_sb", b)][:], ident[:])
+
+        def fin_neg(b):
+            nws = small.tile([P, 1], F32, name="nws", tag="nws")
+            nc.vector.tensor_scalar_mul(out=nws[:], in0=st[("ws", b)][:, 1, 0:1], scalar1=-1.0)
+            st[("nws", b)] = nws
+
+        def fin_out(b):
+            res = respool.tile([P, D], F32, name="res", tag="res")
+            ov = out[b].rearrange("(k c) -> k c", k=K)
+            for h in range(2):
+                cols = slice(STEP * h, STEP * h + STEP)
+                nc.vector.scalar_tensor_tensor(
+                    out=res[:, cols].rearrange("p (q j) -> p q j", j=4),
+                    in0=cent[:, cols].rearrange("p (q j) -> p q j", j=4),
+                    scalar=st[("nws", b)][:, 0:1],
+                    in1=st[("acc", b)][h][:].rearrange("p (j q) -> p q j", j=4),
+                    op0=ALU.mult,
+                    op1=ALU.add,
+                )
+                if b == B - 1:
+                    nc.sync.dma_start(out=ov[:, cols], in_=res[:, cols])
+            if b < B - 1:
+                nc.gpsimd.dma_start(out=ov, in_=res[:])
+
+        warm = const.tile([P, 2], F32)
+        nc.vector.memset(warm[:, 0:1], 0.0)
+        nc.scalar.activation(out=warm[:, 1:2], in_=warm[:, 0:1], func=ACT.Exp)
+        ident = const.tile([P, P], F32)
+        make_identity(nc, ident[:])
+        for ci in range(XBUFS):
+            load(ci)
         nc.gpsimd.dma_start(out=cent[:], in_=centroids)
         cw_w = cw_sb[:].bitcast(F32).rearrange("p (h q i) -> p h i q", h=2, q=P, i=2)
-        cw_t = ps_t.tile([P, 2, 2, P], F32, tag="tr")
+        cw_t = ps_l.tile([P, 2, 2, P], F32, name="cw_t", tag="lg")
         for h in range(2):
             for i in range(2):
                 nc.tensor.transpose(cw_t[:, h, i, :], cw_w[:, h, i, :], ident[:])
@@ -56,126 +289,31 @@ def tile_netvlad_t_kernel(tc, x, conv_w, centroids, out):
         cw_scales = const.tile([P, 2 * K], U8, align_bytes=64)
         nc.vector.quantize_mx(out=cw_codes[:].bitcast(FP8X4), scales=cw_scales[:], in_=cw_g[:])
 
-        for b in range(B):
-            xv = x[b].rearrange("(h p j) a w -> h p j (a w)", h=2, p=P, j=4)
-            widths = [512, 512, 1024, 1024, 1024] if b == 0 else [1024] * 4
-            acc = [
-                ps_a.tile([P, STEP], F32, name="acc0", tag="acc0"),
-                ps_a.tile([P, STEP], F32, name="acc1", tag="acc1"),
-            ]
-            wsum_ps = ps_a.tile([P, K], F32, tag="wsum")
-            n0 = 0
-            for width in widths:
-                xs = xpool.tile([P, 8 * 1024], BF16, tag="xs")
-                xs_b = xs[:, 0 : 8 * width].rearrange("p (c n) -> p c n", c=8)
-                xs_w = xs[:, 0 : 8 * width].bitcast(F32).rearrange("p (c m) -> p c m", c=8)
-                for h in range(2):
-                    nc.sync.dma_start(out=xs_b[:, 4 * h : 4 * h + 4, :], in_=xv[h][:, :, n0 : n0 + width])
-                for o in range(0, width, STEP):
-                    g = (n0 + o) // STEP
-                    g1 = work.tile([P, 2, STEP, 4], BF16, align_bytes=64)
-                    nc.vector.tensor_copy(
-                        out=g1[:, 0].rearrange("p (u e q) j -> p u q j e", u=2, e=2, q=P),
-                        in_=xs_b[:, 0:4, o : o + STEP].rearrange("p j (u q e) -> p u q j e", u=2, e=2, q=P),
-                    )
-                    for u in range(2):
-                        nc.scalar.copy(
-                            out=g1[:, 1, 256 * u : 256 * u + 256, :].rearrange("p (e q) j -> p q j e", e=2, q=P),
-                            in_=xs_b[:, 4:8, o + 256 * u : o + 256 * u + 256].rearrange("p j (q e) -> p q j e", e=2, q=P),
-                        )
-                    c1 = work.tile([P, 2 * STEP], U32, align_bytes=64)
-                    s1 = work.tile([P, 2 * STEP], U8, align_bytes=64)
-                    for h in range(2):
-                        nc.vector.quantize_mx(
-                            out=c1[:, STEP * h : STEP * h + STEP].bitcast(FP8X4),
-                            scales=s1[:, STEP * h : STEP * h + STEP],
-                            in_=g1[:, h].rearrange("p n j -> p (n j)"),
-                        )
-                    lg = ps_l.tile([P, 4, K], F32)
-                    for t in range(4):
-                        for h in range(2):
-                            cols = slice(STEP * h + P * t, STEP * h + P * t + P)
-                            nc.tensor.matmul_mx(
-                                out=lg[:, t, :],
-                                lhsT=c1[:, cols].bitcast(FP8X4),
-                                lhsT_scale=s1[:, cols],
-                                rhs=cw_codes[:, K * h : K * h + K].bitcast(FP8X4),
-                                rhs_scale=cw_scales[:, K * h : K * h + K],
-                                start=(h == 0),
-                                stop=(h == 1),
-                            )
-                    nmx = small.tile([P, 4], F32)
-                    nc.vector.tensor_reduce(out=nmx[:], in_=lg[:], axis=AX.X, op=ALU.max, negate=True)
-                    ex = work.tile([P, 4, K], F32)
-                    ssum = small.tile([P, 4], F32)
-                    for t in range(4):
-                        nc.scalar.activation(
-                            out=ex[:, t, :], in_=lg[:, t, :], func=ACT.Exp,
-                            bias=nmx[:, t : t + 1], scale=1.0, accum_out=ssum[:, t : t + 1],
-                        )
-                    rinv = small.tile([P, 4], F32)
-                    nc.vector.reciprocal(out=rinv[:], in_=ssum[:])
-                    gw = work.tile([P, K, 4], BF16, align_bytes=64)
-                    nc.vector.tensor_tensor(
-                        out=gw[:],
-                        in0=ex[:].rearrange("p t k -> p k t"),
-                        in1=rinv[:].unsqueeze(1).to_broadcast([P, K, 4]),
-                        op=ALU.mult,
-                    )
-                    cq = work.tile([P, K], U32, align_bytes=64)
-                    sq = work.tile([P, K], U8, align_bytes=64)
-                    nc.vector.quantize_mx(
-                        out=cq[:].bitcast(FP8X4), scales=sq[:], in_=gw[:].rearrange("p k t -> p (k t)")
-                    )
-                    for t in range(4):
-                        nc.tensor.matmul(
-                            out=wsum_ps[:],
-                            lhsT=rinv[:, t : t + 1].to_broadcast([P, P]),
-                            rhs=ex[:, t, :],
-                            start=(g == 0 and t == 0),
-                            stop=(g == N // STEP - 1 and t == 3),
-                        )
-                    g2 = work.tile([P, 4 * D], BF16, align_bytes=64)
-                    g2_w = g2[:].bitcast(F32).rearrange("p (c u) -> p c u", u=2)
-                    for i in range(4):
-                        tr = ps_t.tile([P, 2, 2, P], F32, tag="tr")
-                        for u in range(2):
-                            for cb in range(2):
-                                m0 = o // 2 + P * u
-                                nc.tensor.transpose(tr[:, u, cb, :], xs_w[:, 2 * i + cb, m0 : m0 + P], ident[:])
-                        nc.scalar.copy(
-                            out=g2_w[:, 256 * i : 256 * i + 256, :],
-                            in_=tr[:].rearrange("p u c q -> p (c q) u"),
-                        )
-                    c2 = work.tile([P, D], U32, align_bytes=64)
-                    s2 = work.tile([P, D], U8, align_bytes=64)
-                    nc.vector.quantize_mx(out=c2[:].bitcast(FP8X4), scales=s2[:], in_=g2[:])
-                    for h in range(2):
-                        nc.tensor.matmul_mx(
-                            out=acc[h][:],
-                            lhsT=cq[:].bitcast(FP8X4),
-                            lhsT_scale=sq[:],
-                            rhs=c2[:, STEP * h : STEP * h + STEP].bitcast(FP8X4),
-                            rhs_scale=s2[:, STEP * h : STEP * h + STEP],
-                            start=(g == 0),
-                            stop=(g == N // STEP - 1),
-                        )
-                n0 += width
-            ws_sb = small.tile([P, K], F32)
-            nc.vector.tensor_copy(out=ws_sb[:], in_=wsum_ps[:])
-            ws_t = ps_t.tile([P, P], F32, tag="tr")
-            nc.tensor.transpose(ws_t[:], ws_sb[:], ident[:])
-            nws = small.tile([P, 1], F32)
-            nc.vector.tensor_scalar_mul(out=nws[:], in0=ws_t[:, 0:1], scalar1=-1.0)
-            res = respool.tile([P, D], F32)
-            for h in range(2):
-                nc.vector.scalar_tensor_tensor(
-                    out=res[:, STEP * h : STEP * h + STEP].rearrange("p (q j) -> p q j", j=4),
-                    in0=cent[:, STEP * h : STEP * h + STEP].rearrange("p (q j) -> p q j", j=4),
-                    scalar=nws[:, 0:1],
-                    in1=acc[h][:].rearrange("p (j q) -> p q j", j=4),
-                    op0=ALU.mult,
-                    op1=ALU.add,
-                )
-            store = nc.sync if b == B - 1 else nc.gpsimd
-            store.dma_start(out=out[b].rearrange("(k c) -> k c", k=K), in_=res[:])
+        for j in range(-2, NS + 1):
+            closing = j >= 1 and (j - 1) % SPB == SPB - 1
+            b_done = (j - 1) // SPB
+            q1(j)
+            if closing:
+                fin_copy(b_done)
+            mm1(j)
+            if closing and j == NS:
+                fin_tr(b_done)
+            qw(j - 1)
+            q2(j - 1)
+            mm2(j - 1)
+            if closing and j < NS:
+                fin_tr(b_done)
+            vmax(j)
+            sexp(j)
+            tr_r2(j + 1)
+            r1_vector(j + 1)
+            if closing:
+                fin_neg(b_done)
+            r1_scalar(j + 2)
+            norm(j)
+            wsum(j)
+            if closing:
+                fin_out(b_done)
+            for ci in range(len(chunks) - XBUFS):
+                if last_step[ci] - 1 == j:
+                    load(ci + XBUFS)

@@ -21,7 +21,7 @@ STEP = 512
 SPB = N // STEP
 NS = B * SPB
 XBUFS = 5
-VQ = 64
+VQ = 0
 FLOPS = 2 * 2 * B * N * D * K
 
 
@@ -37,7 +37,6 @@ def tile_netvlad_t_kernel(tc, x, conv_w, centroids, out):
         ps_l = ctx.enter_context(tc.psum_pool(name="ps_l", bufs=1))
         ps_t = ctx.enter_context(tc.psum_pool(name="ps_t", bufs=4))
         ps_a = ctx.enter_context(tc.psum_pool(name="ps_a", bufs=1))
-        ctx.enter_context(tc.manual_schedule())
 
         st = {}
         chunks = [(0, 0, 512), (0, 512, 512), (0, 1024, 1024), (0, 2048, 1024), (0, 3072, 1024)]

@@ -21,7 +21,6 @@ STEP = 512
 SPB = N // STEP
 NS = B * SPB
 XBUFS = 5
-VQ = 0
 FLOPS = 2 * 2 * B * N * D * K
 
 
@@ -66,9 +65,9 @@ def tile_netvlad_t_kernel(tc, x, conv_w, centroids, out):
 
         def r1_views(s, h, u):
             ci, o = where[s]
-            dst = st[("g1", s)][:, h, 256 * u : 256 * u + 256, :].rearrange("p (e q) j -> p q j e", e=2, q=P)
+            dst = st[("g1", s)][:, h, 256 * u : 256 * u + 256, :].rearrange("p (e v f) j -> p v j f e", e=2, f=2)
             src = st[("xb", ci)][:, 4 * h : 4 * h + 4, o + 256 * u : o + 256 * u + 256].rearrange(
-                "p j (q e) -> p q j e", e=2, q=P
+                "p j (v f e) -> p v j f e", e=2, f=2
             )
             return dst, src
 
@@ -77,8 +76,7 @@ def tile_netvlad_t_kernel(tc, x, conv_w, centroids, out):
                 return
             st[("g1", s)] = gpool.tile([P, 2, STEP, 4], BF16, name="g1", tag="g1", align_bytes=64)
             dst, src = r1_views(s, 1, 0)
-            if VQ < P:
-                nc.scalar.copy(out=dst[:, VQ:P], in_=src[:, VQ:P])
+            nc.scalar.copy(out=dst, in_=src)
             dst, src = r1_views(s, 1, 1)
             nc.scalar.copy(out=dst, in_=src)
 
@@ -90,9 +88,6 @@ def tile_netvlad_t_kernel(tc, x, conv_w, centroids, out):
                 out=st[("g1", s)][:, 0].rearrange("p (u e q) j -> p u q j e", u=2, e=2, q=P),
                 in_=st[("xb", ci)][:, 0:4, o : o + STEP].rearrange("p j (u q e) -> p u q j e", u=2, e=2, q=P),
             )
-            if VQ > 0:
-                dst, src = r1_views(s, 1, 0)
-                nc.vector.tensor_copy(out=dst[:, 0:VQ], in_=src[:, 0:VQ])
 
         def q1(s):
             if not 0 <= s < NS:

@@ -283,19 +283,19 @@ def tile_netvlad_t_kernel(tc, x, conv_w, centroids, out):
         cw_scales = const.tile([P, 2 * K], U8, align_bytes=64)
         nc.vector.quantize_mx(out=cw_codes[:].bitcast(FP8X4), scales=cw_scales[:], in_=cw_g[:])
 
+        ctx.enter_context(tc.manual_schedule(engines={mybir.EngineType.PE}))
         for j in range(-2, NS + 1):
             closing = j >= 1 and (j - 1) % SPB == SPB - 1
             b_done = (j - 1) // SPB
             q1(j)
+            mm1(j)
+            wsum(j - 1)
             if closing:
                 fin_copy(b_done)
-            mm1(j)
-            if closing and j == NS:
-                fin_tr(b_done)
             qw(j - 1)
             q2(j - 1)
             mm2(j - 1)
-            if closing and j < NS:
+            if closing:
                 fin_tr(b_done)
             vmax(j)
             sexp(j)
@@ -305,7 +305,6 @@ def tile_netvlad_t_kernel(tc, x, conv_w, centroids, out):
                 fin_neg(b_done)
             r1_scalar(j + 2)
             norm(j)
-            wsum(j)
             if closing:
                 fin_out(b_done)
             for ci in range(len(chunks) - XBUFS):

@@ -289,22 +289,22 @@ def tile_netvlad_t_kernel(tc, x, conv_w, centroids, out):
             b_done = (j - 1) // SPB
             q1(j)
             mm1(j)
+            qw(j - 1)
+            q2(j - 1)
+            vmax(j)
+            sexp(j)
+            norm(j)
+            tr_r2(j + 1)
             wsum(j - 1)
             if closing:
                 fin_copy(b_done)
-            qw(j - 1)
-            q2(j - 1)
             mm2(j - 1)
             if closing:
                 fin_tr(b_done)
-            vmax(j)
-            sexp(j)
-            tr_r2(j + 1)
             r1_vector(j + 1)
             if closing:
                 fin_neg(b_done)
             r1_scalar(j + 2)
-            norm(j)
             if closing:
                 fin_out(b_done)
             for ci in range(len(chunks) - XBUFS):

from contextlib import ExitStack

import concourse.mybir as mybir
from concourse.masks import make_identity

F32 = mybir.dt.float32
BF16 = mybir.dt.bfloat16
U32 = mybir.dt.uint32
U8 = mybir.dt.uint8
FP8X4 = mybir.dt.float8_e4m3fn_x4
ALU = mybir.AluOpType
ACT = mybir.ActivationFunctionType
AX = mybir.AxisListType

P = 128
B = 4
D = 1024
N = 4096
K = 128
STEP = 512
SPB = N // STEP
NS = B * SPB
XBUFS = 5
FLOPS = 2 * 2 * B * N * D * K


def tile_netvlad_t_kernel(tc, x, conv_w, centroids, out):
    nc = tc.nc
    with ExitStack() as ctx:
        const = ctx.enter_context(tc.tile_pool(name="const", bufs=1))
        xpool = ctx.enter_context(tc.tile_pool(name="xpool", bufs=XBUFS))
        gpool = ctx.enter_context(tc.tile_pool(name="gpool", bufs=3))
        qpool = ctx.enter_context(tc.tile_pool(name="qpool", bufs=2))
        small = ctx.enter_context(tc.tile_pool(name="small", bufs=3))
        respool = ctx.enter_context(tc.tile_pool(name="respool", bufs=2))
        ps_l = ctx.enter_context(tc.psum_pool(name="ps_l", bufs=1))
        ps_t = ctx.enter_context(tc.psum_pool(name="ps_t", bufs=4))
        ps_a = ctx.enter_context(tc.psum_pool(name="ps_a", bufs=1))

        st = {}
        chunks = [(0, 0, 512), (0, 512, 512), (0, 1024, 1024), (0, 2048, 1024), (0, 3072, 1024)]
        for b in range(1, B):
            chunks.extend([(b, n0, 1024) for n0 in range(0, N, 1024)])
        where = {}
        last_step = {}
        for ci, (b, n0, width) in enumerate(chunks):
            for o in range(0, width, STEP):
                where[b * SPB + (n0 + o) // STEP] = (ci, o)
                last_step[ci] = b * SPB + (n0 + o) // STEP

        cw_sb = const.tile([P, D], BF16)
        cent = const.tile([P, D], BF16)

        def load(ci):
            b, n0, width = chunks[ci]
            xv = x[b].rearrange("(h p j) a w -> h p j (a w)", h=2, p=P, j=4)
            xs = xpool.tile([P, 8 * 1024], BF16, name="xs", tag="xs")
            xs_b = xs[:, 0 : 8 * width].rearrange("p (c n) -> p c n", c=8)
            for h in (1, 0):
                nc.sync.dma_start(out=xs_b[:, 4 * h : 4 * h + 4, :], in_=xv[h][:, :, n0 : n0 + width])
                if ci == 0 and h == 1:
                    nc.sync.dma_start(out=cw_sb[:], in_=conv_w)
            st[("xb", ci)] = xs_b
            st[("xw", ci)] = xs[:, 0 : 8 * width].bitcast(F32).rearrange("p (c m) -> p c m", c=8)

        def r1_views(s, h, u):
            ci, o = where[s]
            dst = st[("g1", s)][:, h, 256 * u : 256 * u + 256, :].rearrange("p (e v f) j -> p v j f e", e=2, f=2)
            src = st[("xb", ci)][:, 4 * h : 4 * h + 4, o + 256 * u : o + 256 * u + 256].rearrange(
                "p j (v f e) -> p v j f e", e=2, f=2
            )
            return dst, src

        def r1_scalar(s):
            if not 0 <= s < NS:
                return
            st[("g1", s)] = gpool.tile([P, 2, STEP, 4], BF16, name="g1", tag="g1", align_bytes=64)
            dst, src = r1_views(s, 1, 0)
            nc.scalar.copy(out=dst, in_=src)
            dst, src = r1_views(s, 1, 1)
            nc.scalar.copy(out=dst, in_=src)

        def r1_vector(s):
            if not 0 <= s < NS:
                return
            ci, o = where[s]
            nc.vector.tensor_copy(
                out=st[("g1", s)][:, 0].rearrange("p (u e q) j -> p u q j e", u=2, e=2, q=P),
                in_=st[("xb", ci)][:, 0:4, o : o + STEP].rearrange("p j (u q e) -> p u q j e", u=2, e=2, q=P),
            )

        def q1(s):
            if not 0 <= s < NS:
                return
            c1 = qpool.tile([P, 2 * STEP], U32, name="c1", tag="c1", align_bytes=64)
            s1 = qpool.tile([P, 2 * STEP], U8, name="s1", tag="s1", align_bytes=64)
            for h in range(2):
                nc.vector.quantize_mx(
                    out=c1[:, STEP * h : STEP * h + STEP].bitcast(FP8X4),
                    scales=s1[:, STEP * h : STEP * h + STEP],
                    in_=st[("g1", s)][:, h].rearrange("p n j -> p (n j)"),
                )
            st[("c1", s)] = (c1, s1)

        def mm1(s):
            if not 0 <= s < NS:
                return
            c1, s1 = st[("c1", s)]
            lg = ps_l.tile([P, 4, K], F32, name="lg", tag="lg")
            for t in range(4):
                for h in range(2):
                    cols = slice(STEP * h + P * t, STEP * h + P * t + P)
                    nc.tensor.matmul_mx(
                        out=lg[:, t, :],
                        lhsT=c1[:, cols].bitcast(FP8X4),
                        lhsT_scale=s1[:, cols],
                        rhs=cw_codes[:, K * h : K * h + K].bitcast(FP8X4),
                        rhs_scale=cw_scales[:, K * h : K * h + K],
                        start=(h == 0),
                        stop=(h == 1),
                    )
            st[("lg", s)] = lg

        def vmax(s):
            if not 0 <= s < NS:
                return
            nmx = small.tile([P, 4], F32, name="nmx", tag="nmx")
            nc.vector.tensor_reduce(out=nmx[:], in_=st[("lg", s)][:], axis=AX.X, op=ALU.max, negate=True)
            st[("nmx", s)] = nmx

        def sexp(s):
            if not 0 <= s < NS:
                return
            ex = qpool.tile([P, 4, K], F32, name="ex", tag="ex")
            ssum = small.tile([P, 4], F32, name="ssum", tag="ssum")
            for t in range(4):
                nc.scalar.activation(
                    out=ex[:, t, :], in_=st[("lg", s)][:, t, :], func=ACT.Exp,
                    bias=st[("nmx", s)][:, t : t + 1], scale=1.0, accum_out=ssum[:, t : t + 1],
                )
            st[("ex", s)] = (ex, ssum)

        def norm(s):
            if not 0 <= s < NS:
                return
            ex, ssum = st[("ex", s)]
            rinv = small.tile([P, 4], F32, name="rinv", tag="rinv")
            nc.vector.reciprocal(out=rinv[:], in_=ssum[:])
            gw = qpool.tile([P, K, 4], BF16, name="gw", tag="gw", align_bytes=64)
            nc.vector.tensor_tensor(
                out=gw[:],
                in0=ex[:].rearrange("p t k -> p k t"),
                in1=rinv[:].unsqueeze(1).to_broadcast([P, K, 4]),
                op=ALU.mult,
            )
            st[("gw", s)] = (gw, rinv)

        def qw(s):
            if not 0 <= s < NS:
                return
            cq = qpool.tile([P, K], U32, name="cq", tag="cq", align_bytes=64)
            sq = qpool.tile([P, K], U8, name="sq", tag="sq", align_bytes=64)
            nc.vector.quantize_mx(
                out=cq[:].bitcast(FP8X4), scales=sq[:], in_=st[("gw", s)][0][:].rearrange("p k t -> p (k t)")
            )
            st[("cq", s)] = (cq, sq)

        def wsum(s):
            if not 0 <= s < NS:
                return
            b, g = divmod(s, SPB)
            if g == 0:
                st[("ws", b)] = ps_a.tile([P, 2, K], F32, name="ws", tag="ws")
            ex = st[("ex", s)][0]
            rinv = st[("gw", s)][1]
            for t in range(4):
                nc.tensor.matmul(
                    out=st[("ws", b)][:, 0, :],
                    lhsT=rinv[:, t : t + 1].to_broadcast([P, P]),
                    rhs=ex[:, t, :],
                    start=(g == 0 and t == 0),
                    stop=(g == SPB - 1 and t == 3),
                )

        def tr_r2(s):
            if not 0 <= s < NS:
                return
            ci, o = where[s]
            xs_w = st[("xw", ci)]
            g2 = gpool.tile([P, 4 * D], BF16, name="g2", tag="g2", align_bytes=64)
            g2_w = g2[:].bitcast(F32).rearrange("p (c u) -> p c u", u=2)
            for i in range(4):
                tr = ps_t.tile([P, 2, 2, P], F32, name="tr", tag="tr")
                for u in range(2):
                    for cb in range(2):
                        m0 = o // 2 + P * u
                        nc.tensor.transpose(tr[:, u, cb, :], xs_w[:, 2 * i + cb, m0 : m0 + P], ident[:])
                nc.scalar.copy(
                    out=g2_w[:, 256 * i : 256 * i + 256, :], in_=tr[:].rearrange("p u c q -> p (c q) u")
                )
            st[("g2", s)] = g2

        def q2(s):
            if not 0 <= s < NS:
                return
            c2 = qpool.tile([P, D], U32, name="c2", tag="c2", align_bytes=64)
            s2 = qpool.tile([P, D], U8, name="s2", tag="s2", align_bytes=64)
            nc.vector.quantize_mx(out=c2[:].bitcast(FP8X4), scales=s2[:], in_=st[("g2", s)][:])
            st[("c2", s)] = (c2, s2)

        def mm2(s):
            if not 0 <= s < NS:
                return
            b, g = divmod(s, SPB)
            if g == 0:
                st[("acc", b)] = [
                    ps_a.tile([P, STEP], F32, name="acc0", tag="acc0"),
                    ps_a.tile([P, STEP], F32, name="acc1", tag="acc1"),
                ]
            cq, sq = st[("cq", s)]
            c2, s2 = st[("c2", s)]
            for h in range(2):
                nc.tensor.matmul_mx(
                    out=st[("acc", b)][h][:],
                    lhsT=cq[:].bitcast(FP8X4),
                    lhsT_scale=sq[:],
                    rhs=c2[:, STEP * h : STEP * h + STEP].bitcast(FP8X4),
                    rhs_scale=s2[:, STEP * h : STEP * h + STEP],
                    start=(g == 0),
                    stop=(g == SPB - 1),
                )

        def fin_copy(b):
            ws_sb = small.tile([P, K], F32, name="ws_sb", tag="ws_sb")
            nc.vector.tensor_copy(out=ws_sb[:], in_=st[("ws", b)][:, 0, :])
            st[("ws_sb", b)] = ws_sb

        def fin_tr(b):
            nc.tensor.transpose(st[("ws", b)][:, 1, :], st[("ws_sb", b)][:], ident[:])

        def fin_neg(b):
            nws = small.tile([P, 1], F32, name="nws", tag="nws")
            nc.vector.tensor_scalar_mul(out=nws[:], in0=st[("ws", b)][:, 1, 0:1], scalar1=-1.0)
            st[("nws", b)] = nws

        def fin_out(b):
            res = respool.tile([P, D], F32, name="res", tag="res")
            ov = out[b].rearrange("(k c) -> k c", k=K)
            for h in range(2):
                cols = slice(STEP * h, STEP * h + STEP)
                nc.vector.scalar_tensor_tensor(
                    out=res[:, cols].rearrange("p (q j) -> p q j", j=4),
                    in0=cent[:, cols].rearrange("p (q j) -> p q j", j=4),
                    scalar=st[("nws", b)][:, 0:1],
                    in1=st[("acc", b)][h][:].rearrange("p (j q) -> p q j", j=4),
                    op0=ALU.mult,
                    op1=ALU.add,
                )
                if b == B - 1:
                    nc.sync.dma_start(out=ov[:, cols], in_=res[:, cols])
            if b < B - 1:
                nc.gpsimd.dma_start(out=ov, in_=res[:])

        warm = const.tile([P, 2], F32)
        nc.vector.memset(warm[:, 0:1], 0.0)
        nc.scalar.activation(out=warm[:, 1:2], in_=warm[:, 0:1], func=ACT.Exp)
        ident = const.tile([P, P], F32)
        make_identity(nc, ident[:])
        for ci in range(XBUFS):
            load(ci)
        nc.gpsimd.dma_start(out=cent[:], in_=centroids)
        cw_w = cw_sb[:].bitcast(F32).rearrange("p (h q i) -> p h i q", h=2, q=P, i=2)
        cw_t = ps_l.tile([P, 2, 2, P], F32, name="cw_t", tag="lg")
        for h in range(2):
            for i in range(2):
                nc.tensor.transpose(cw_t[:, h, i, :], cw_w[:, h, i, :], ident[:])
        cw_g = const.tile([P, D], BF16, align_bytes=64)
        nc.vector.tensor_copy(
            out=cw_g[:].bitcast(F32).rearrange("p (h k i) -> p h k i", h=2, k=K, i=2),
            in_=cw_t[:].rearrange("p h i k -> p h k i"),
        )
        cw_codes = const.tile([P, 2 * K], U32, align_bytes=64)
        cw_scales = const.tile([P, 2 * K], U8, align_bytes=64)
        nc.vector.quantize_mx(out=cw_codes[:].bitcast(FP8X4), scales=cw_scales[:], in_=cw_g[:])

        ctx.enter_context(tc.manual_schedule(engines={mybir.EngineType.PE}))
        for j in range(-2, NS + 1):
            closing = j >= 1 and (j - 1) % SPB == SPB - 1
            b_done = (j - 1) // SPB
            q1(j)
            mm1(j)
            qw(j - 1)
            q2(j - 1)
            vmax(j)
            sexp(j)
            norm(j)
            tr_r2(j + 1)
            wsum(j - 1)
            if closing:
                fin_copy(b_done)
            mm2(j - 1)
            if closing:
                fin_tr(b_done)
            r1_vector(j + 1)
            if closing:
                fin_neg(b_done)
            r1_scalar(j + 2)
            if closing:
                fin_out(b_done)
            for ci in range(len(chunks) - XBUFS):
                if last_step[ci] - 1 == j:
                    load(ci + XBUFS)
